import numpy as np
import ml_dtypes


def mxq(x, axis, fmt="e4m3"):
    dtype, down = {"e4m3": (ml_dtypes.float8_e4m3fn, 7), "e5m2": (ml_dtypes.float8_e5m2, 14)}[fmt]
    v = np.moveaxis(np.asarray(x, np.float32).astype(ml_dtypes.bfloat16).astype(np.float64), axis, -1)
    blocks = v.reshape(v.shape[:-1] + (-1, 32))
    amax = np.abs(blocks).max(-1, keepdims=True)
    byte = np.maximum(np.where(amax > 0, np.frexp(amax)[1] - 1 + 127, 0) - down, 1)
    scale = np.exp2(byte - 127.0)
    codes = (blocks / scale).astype(np.float32).astype(dtype).astype(np.float64)
    return np.moveaxis((codes * scale).reshape(v.shape), -1, axis)


WIDE = False


def mx_kscale(k):
    if not WIDE:
        return np.ones(k)
    levels = np.array([10, -10, 5, -5, 0])
    a = np.random.permutation(np.resize(levels, k // 512 * 4)).reshape(k // 512, 4)
    idx = np.arange(k)
    return np.exp2(a[idx // 512, idx % 128 // 32])


BF16 = ml_dtypes.bfloat16


def bf(x):
    return np.asarray(x, np.float32).astype(BF16)


def f64(x):
    return np.asarray(x).astype(np.float64)


B, F, N = 2, 512, 2048


def setup_inputs():
    t = mx_kscale(N)
    u = t / t.min()
    amp = np.random.uniform(0.5, 1.5, (B, 1, N))
    emb = np.random.uniform(1e-3, 1.0, (B, F, N)) * amp * np.sqrt(5.0 / F)
    mom = np.random.uniform(0.2, 1.0, (B, N))
    alpha_p = bf(0.6 + 0.3 * np.random.uniform(size=(1, 1)))
    beta_p = bf(1.15 + 0.2 * np.random.uniform(size=(1, 1, 1)))
    a = float(f64(alpha_p)[0, 0])
    emb = emb * u[None, None, :]
    emb[:, 4, :] = mom * u[None, :] ** (-1.0 / a)
    return {"emb": bf(emb), "alpha_p": alpha_p, "beta_p": beta_p}


def reference(emb, alpha_p, beta_p):
    e = f64(emb)
    sq_norms = np.sum(e * e, axis=1)
    eq = mxq(e, 1, "e4m3")
    gram = eq.transpose(0, 2, 1) @ eq
    sqdist = sq_norms[:, :, None] + sq_norms[:, None, :] - 2.0 * gram
    momentum = e[:, 4, :]
    alpha = f64(alpha_p)[0, 0]
    pow_momenta = np.exp(2.0 * alpha * np.log(momentum))
    min_momenta = np.minimum(pow_momenta[:, :, None], pow_momenta[:, None, :])
    d_ij = sqdist * min_momenta
    beta_sq = f64(beta_p)[0, 0, 0] ** 2
    return np.exp(-beta_sq * d_ij)

@@ -1,0 +1,224 @@
+from contextlib import ExitStack
+
+from concourse import mybir
+from concourse.masks import make_identity
+
+F32 = mybir.dt.float32
+BF16 = mybir.dt.bfloat16
+U32 = mybir.dt.uint32
+U8 = mybir.dt.uint8
+FP8X4 = mybir.dt.float8_e4m3fn_x4
+ALU = mybir.AluOpType
+ACT = mybir.ActivationFunctionType
+
+BATCH = 2
+FEATURES = 512
+PARTICLES = 2048
+MOMENTUM_FEATURE = 4
+
+P = 128
+PACK = 4
+CHUNK = 512
+BLOCKS = CHUNK // P
+CHUNKS = PARTICLES // CHUNK
+ROW_TILES = PARTICLES // P
+SCALAR_COLUMNS = 256
+
+FLOPS = 2 * BATCH * PARTICLES * PARTICLES * FEATURES
+
+assert FEATURES == P * PACK
+
+
+def tile_qcdawareold_kernel(tc, emb, alpha_p, beta_p, out):
+    nc = tc.nc
+    with ExitStack() as ctx:
+        keep = ctx.enter_context(tc.tile_pool(name="keep", bufs=1))
+        stage = ctx.enter_context(tc.tile_pool(name="stage", bufs=3))
+        exponents = ctx.enter_context(tc.tile_pool(name="exponents", bufs=2 * BLOCKS))
+        results = ctx.enter_context(tc.tile_pool(name="results", bufs=6))
+        mirrors = ctx.enter_context(tc.tile_pool(name="mirrors", bufs=3 * BLOCKS))
+        psum_gram = ctx.enter_context(tc.psum_pool(name="psum_gram", bufs=3))
+        psum_mirror = ctx.enter_context(tc.psum_pool(name="psum_mirror", bufs=3))
+        psum_prepare = ctx.enter_context(tc.psum_pool(name="psum_prepare", bufs=2))
+
+        ident_f32 = keep.tile([P, P], F32, name="ident_f32")
+        make_identity(nc, ident_f32[:])
+        ident_bf16 = keep.tile([P, P], BF16, name="ident_bf16")
+        make_identity(nc, ident_bf16[:])
+
+        alpha_bf16 = keep.tile([P, 1], BF16, name="alpha_bf16")
+        nc.scalar.dma_start(out=alpha_bf16[:], in_=alpha_p.rearrange("a b -> (a b)").partition_broadcast(P))
+        beta_bf16 = keep.tile([P, 1], BF16, name="beta_bf16")
+        nc.scalar.dma_start(out=beta_bf16[:], in_=beta_p.rearrange("a b c -> (a b c)").partition_broadcast(P))
+
+        momentum_rows = keep.tile([P, P], BF16, name="momentum_rows")
+        nc.vector.memset(momentum_rows[:], 0.0)
+        for b in range(BATCH):
+            nc.scalar.dma_start(
+                out=momentum_rows[b * ROW_TILES : (b + 1) * ROW_TILES, :],
+                in_=emb[b, MOMENTUM_FEATURE, :].rearrange("(t p) -> t p", p=P),
+            )
+
+        raw = [[None] * CHUNKS for b in range(BATCH)]
+        for b in range(BATCH):
+            rows = emb[b].rearrange("(p t) w -> p t w", t=PACK)
+            for c in range(CHUNKS):
+                raw[b][c] = keep.tile([P, PACK, CHUNK], BF16, name="raw%d%d" % (b, c))
+                nc.sync.dma_start(out=raw[b][c][:], in_=rows[:, :, c * CHUNK : (c + 1) * CHUNK])
+
+        two_alpha = keep.tile([P, 1], F32, name="two_alpha")
+        nc.vector.tensor_scalar(
+            out=two_alpha[:], in0=alpha_bf16[:], scalar1=2.0, scalar2=None, op0=ALU.mult
+        )
+        beta_f32 = keep.tile([P, 1], F32, name="beta_f32")
+        nc.vector.tensor_copy(out=beta_f32[:], in_=beta_bf16[:])
+        two_beta_sq = keep.tile([P, 1], F32, name="two_beta_sq")
+        nc.vector.tensor_scalar(
+            out=two_beta_sq[:], in0=beta_f32[:], scalar1=beta_f32[:, 0:1], scalar2=2.0,
+            op0=ALU.mult, op1=ALU.mult,
+        )
+        momentum_cols = psum_prepare.tile([P, P], BF16, name="momentum_cols", tag="prepare")
+        nc.tensor.transpose(momentum_cols[:], momentum_rows[:], ident_bf16[:])
+        log_momentum = keep.tile([P, BATCH * ROW_TILES], F32, name="log_momentum")
+        nc.scalar.activation(out=log_momentum[:], in_=momentum_cols[:, 0 : BATCH * ROW_TILES], func=ACT.Ln)
+        power = keep.tile([P, BATCH * ROW_TILES], F32, name="power")
+        nc.scalar.activation(out=power[:], in_=log_momentum[:], func=ACT.Exp, scale=two_alpha[:, 0:1])
+        p_col = keep.tile([P, BATCH * ROW_TILES], F32, name="p_col")
+        nc.vector.tensor_scalar(
+            out=p_col[:], in0=power[:], scalar1=two_beta_sq[:, 0:1], scalar2=None, op0=ALU.mult
+        )
+
+        codes = [[None] * CHUNKS for b in range(BATCH)]
+        scales = [[None] * CHUNKS for b in range(BATCH)]
+        h_col = [[None] * CHUNKS for b in range(BATCH)]
+        h_row = [[None] * CHUNKS for b in range(BATCH)]
+        p_row = [[None] * CHUNKS for b in range(BATCH)]
+
+        def spread(column_of_block, name):
+            bank = psum_prepare.tile([P, CHUNK], F32, name="bank", tag="prepare")
+            for q in range(BLOCKS):
+                nc.tensor.transpose(
+                    bank[:, q * P : (q + 1) * P], column_of_block(q).to_broadcast([P, P]), ident_f32[:]
+                )
+            row = keep.tile([P, CHUNK], F32, name=name)
+            nc.scalar.copy(out=row[:], in_=bank[:])
+            return row
+
+        def prepare_chunk(b, c):
+            source = raw[b][c]
+            grouped = stage.tile([P, CHUNK, PACK], BF16, name="grouped", align_bytes=64)
+            split = CHUNK - SCALAR_COLUMNS
+            nc.vector.tensor_copy(
+                out=grouped[:, 0:split, :].rearrange("p (c i) t -> p c t i", i=4),
+                in_=source[:, :, 0:split].rearrange("p t (c i) -> p c t i", i=4),
+            )
+            nc.scalar.copy(
+                out=grouped[:, split:CHUNK, :].rearrange("p (c i) t -> p c t i", i=4),
+                in_=source[:, :, split:CHUNK].rearrange("p t (c i) -> p c t i", i=4),
+            )
+
+            norms = psum_prepare.tile([P, CHUNK], F32, name="norms", tag="prepare")
+            for q in range(BLOCKS):
+                for t in range(PACK):
+                    block = source[:, t, q * P : (q + 1) * P]
+                    nc.tensor.matmul(
+                        norms[:, q * P : (q + 1) * P], lhsT=block, rhs=block,
+                        start=(t == 0), stop=(t == PACK - 1),
+                    )
+            h_col[b][c] = keep.tile([P, BLOCKS], F32, name="h_col%d%d" % (b, c))
+            masked = stage.tile([P, CHUNK], F32, name="masked")
+            for q in range(BLOCKS):
+                nc.vector.scalar_tensor_tensor(
+                    out=masked[:, q * P : (q + 1) * P], in0=norms[:, q * P : (q + 1) * P], scalar=0.5,
+                    in1=ident_f32[:], op0=ALU.mult, op1=ALU.mult, accum_out=h_col[b][c][:, q : q + 1],
+                )
+
+            codes[b][c] = keep.tile([P, CHUNK], U32, name="codes%d%d" % (b, c), align_bytes=64)
+            scales[b][c] = keep.tile([P, CHUNK], U8, name="scales%d%d" % (b, c), align_bytes=64)
+            nc.vector.quantize_mx(
+                out=codes[b][c][:].bitcast(FP8X4),
+                scales=scales[b][c][:],
+                in_=grouped[:].rearrange("p w t -> p (w t)"),
+            )
+
+            first = b * ROW_TILES + c * BLOCKS
+            h_row[b][c] = spread(lambda q: h_col[b][c][:, q : q + 1], "h_row%d%d" % (b, c))
+            p_row[b][c] = spread(lambda q: p_col[:, first + q : first + q + 1], "p_row%d%d" % (b, c))
+
+        def half_distance(b, a, r, c, lo):
+            gram = psum_gram.tile([P, CHUNK], F32, name="gram")
+            nc.tensor.matmul_mx(
+                out=gram[:],
+                lhsT=codes[b][a][:, r * P : (r + 1) * P].bitcast(FP8X4),
+                lhsT_scale=scales[b][a][:, r * P : (r + 1) * P],
+                rhs=codes[b][c][:].bitcast(FP8X4),
+                rhs_scale=scales[b][c][:],
+                start=True,
+                stop=True,
+            )
+            x = exponents.tile([P, CHUNK], F32, name="x")
+            nc.vector.scalar_tensor_tensor(
+                out=x[:, lo:], in0=gram[:, lo:], scalar=h_col[b][a][:, r : r + 1], in1=h_row[b][c][:, lo:],
+                op0=ALU.subtract, op1=ALU.subtract,
+            )
+            return x
+
+        def weigh(b, a, r, c, lo, x):
+            i = b * ROW_TILES + a * BLOCKS + r
+            nc.vector.scalar_tensor_tensor(
+                out=x[:, lo:], in0=p_row[b][c][:, lo:], scalar=p_col[:, i : i + 1], in1=x[:, lo:],
+                op0=ALU.min, op1=ALU.mult,
+            )
+
+        def unit(b, a, c, mirror, at):
+            diagonal = a == c
+
+            def finish(r, x):
+                lo = r * P if diagonal else 0
+                weigh(b, a, r, c, lo, x)
+                if diagonal:
+                    nc.scalar.activation(out=mirror[r][:, at + lo : at + CHUNK], in_=x[:, lo:], func=ACT.Exp)
+                else:
+                    direct = results.tile([P, CHUNK], F32, name="direct")
+                    nc.scalar.activation(out=direct[:], in_=x[:], func=ACT.Exp)
+                    row0 = (a * BLOCKS + r) * P
+                    nc.sync.dma_start(out=out[b, row0 : row0 + P, c * CHUNK : (c + 1) * CHUNK], in_=direct[:])
+
+            xs = []
+            for r in range(BLOCKS):
+                xs.append(half_distance(b, a, r, c, r * P if diagonal else 0))
+                if r > 0:
+                    finish(r - 1, xs[r - 1])
+            finish(BLOCKS - 1, xs[BLOCKS - 1])
+
+            for q in range(1 if diagonal else 0, BLOCKS):
+                sources = q if diagonal else BLOCKS
+                flipped = psum_mirror.tile([P, CHUNK], F32, name="flipped")
+                for r in range(sources):
+                    nc.tensor.transpose(
+                        flipped[:, r * P : (r + 1) * P], xs[r][:, q * P : (q + 1) * P], ident_f32[:]
+                    )
+                nc.scalar.activation(
+                    out=mirror[q][:, at : at + sources * P], in_=flipped[:, 0 : sources * P], func=ACT.Exp
+                )
+
+        def column_step(b, c):
+            for a in range(c + 1):
+                if a % 2 == 0:
+                    mirror = [mirrors.tile([P, 2 * CHUNK], F32, name="mirror") for q in range(BLOCKS)]
+                unit(b, a, c, mirror, (a % 2) * CHUNK)
+                if a % 2 == 1 or a == c:
+                    col0 = (a - a % 2) * CHUNK
+                    width = (a % 2 + 1) * CHUNK
+                    for q in range(BLOCKS):
+                        row0 = (c * BLOCKS + q) * P
+                        nc.sync.dma_start(
+                            out=out[b, row0 : row0 + P, col0 : col0 + width], in_=mirror[q][:, 0:width]
+                        )
+
+        steps = [(b, c) for b in range(BATCH) for c in range(CHUNKS)]
+        prepare_chunk(*steps[0])
+        for s in range(len(steps)):
+            if s + 1 < len(steps):
+                prepare_chunk(*steps[s + 1])
+            column_step(*steps[s])

@@ -22,7 +22,6 @@ CHUNK = 512
 BLOCKS = CHUNK // P
 CHUNKS = PARTICLES // CHUNK
 ROW_TILES = PARTICLES // P
-SCALAR_COLUMNS = 256
 
 FLOPS = 2 * BATCH * PARTICLES * PARTICLES * FEATURES
 
@@ -33,13 +32,14 @@ def tile_qcdawareold_kernel(tc, emb, alpha_p, beta_p, out):
     nc = tc.nc
     with ExitStack() as ctx:
         keep = ctx.enter_context(tc.tile_pool(name="keep", bufs=1))
-        stage = ctx.enter_context(tc.tile_pool(name="stage", bufs=3))
-        exponents = ctx.enter_context(tc.tile_pool(name="exponents", bufs=2 * BLOCKS))
-        results = ctx.enter_context(tc.tile_pool(name="results", bufs=6))
-        mirrors = ctx.enter_context(tc.tile_pool(name="mirrors", bufs=3 * BLOCKS))
-        psum_gram = ctx.enter_context(tc.psum_pool(name="psum_gram", bufs=3))
+        stage = ctx.enter_context(tc.tile_pool(name="stage", bufs=1))
+        exponents = ctx.enter_context(tc.tile_pool(name="exponents", bufs=3 * BLOCKS))
+        results = ctx.enter_context(tc.tile_pool(name="results", bufs=8))
+        mirrors = ctx.enter_context(tc.tile_pool(name="mirrors", bufs=4 * BLOCKS))
+        psum_gram = ctx.enter_context(tc.psum_pool(name="psum_gram", bufs=2))
         psum_mirror = ctx.enter_context(tc.psum_pool(name="psum_mirror", bufs=3))
-        psum_prepare = ctx.enter_context(tc.psum_pool(name="psum_prepare", bufs=2))
+        psum_prepare = ctx.enter_context(tc.psum_pool(name="psum_prepare", bufs=1))
+        psum_p_row = ctx.enter_context(tc.psum_pool(name="psum_p_row", bufs=2))
 
         ident_f32 = keep.tile([P, P], F32, name="ident_f32")
         make_identity(nc, ident_f32[:])
@@ -94,28 +94,25 @@ def tile_qcdawareold_kernel(tc, emb, alpha_p, beta_p, out):
         h_row = [[None] * CHUNKS for b in range(BATCH)]
         p_row = [[None] * CHUNKS for b in range(BATCH)]
 
-        def spread(column_of_block, name):
-            bank = psum_prepare.tile([P, CHUNK], F32, name="bank", tag="prepare")
+        def spread(bank, column_of_block):
             for q in range(BLOCKS):
                 nc.tensor.transpose(
                     bank[:, q * P : (q + 1) * P], column_of_block(q).to_broadcast([P, P]), ident_f32[:]
                 )
-            row = keep.tile([P, CHUNK], F32, name=name)
-            nc.scalar.copy(out=row[:], in_=bank[:])
-            return row
 
         def prepare_chunk(b, c):
             source = raw[b][c]
             grouped = stage.tile([P, CHUNK, PACK], BF16, name="grouped", align_bytes=64)
-            split = CHUNK - SCALAR_COLUMNS
-            nc.vector.tensor_copy(
-                out=grouped[:, 0:split, :].rearrange("p (c i) t -> p c t i", i=4),
-                in_=source[:, :, 0:split].rearrange("p t (c i) -> p c t i", i=4),
-            )
-            nc.scalar.copy(
-                out=grouped[:, split:CHUNK, :].rearrange("p (c i) t -> p c t i", i=4),
-                in_=source[:, :, split:CHUNK].rearrange("p t (c i) -> p c t i", i=4),
-            )
+            if (b, c) == (0, 0):
+                nc.vector.tensor_copy(
+                    out=grouped[:].rearrange("p (c i) t -> p c t i", i=4),
+                    in_=source[:].rearrange("p t (c i) -> p c t i", i=4),
+                )
+            else:
+                nc.gpsimd.tensor_scalar(
+                    out=grouped[:], in0=source[:].rearrange("p t w -> p w t"), scalar1=1.0, scalar2=0.0,
+                    op0=ALU.mult, op1=ALU.add,
+                )
 
             norms = psum_prepare.tile([P, CHUNK], F32, name="norms", tag="prepare")
             for q in range(BLOCKS):
@@ -142,8 +139,12 @@ def tile_qcdawareold_kernel(tc, emb, alpha_p, beta_p, out):
             )
 
             first = b * ROW_TILES + c * BLOCKS
-            h_row[b][c] = spread(lambda q: h_col[b][c][:, q : q + 1], "h_row%d%d" % (b, c))
-            p_row[b][c] = spread(lambda q: p_col[:, first + q : first + q + 1], "p_row%d%d" % (b, c))
+            h_bank = psum_prepare.tile([P, CHUNK], F32, name="h_bank", tag="prepare")
+            spread(h_bank, lambda q: h_col[b][c][:, q : q + 1])
+            h_row[b][c] = keep.tile([P, CHUNK], F32, name="h_row%d%d" % (b, c))
+            nc.scalar.copy(out=h_row[b][c][:], in_=h_bank[:])
+            p_row[b][c] = psum_p_row.tile([P, CHUNK], F32, name="p_row")
+            spread(p_row[b][c], lambda q: p_col[:, first + q : first + q + 1])
 
         def half_distance(b, a, r, c, lo):
             gram = psum_gram.tile([P, CHUNK], F32, name="gram")

@@ -22,6 +22,9 @@ CHUNK = 512
 BLOCKS = CHUNK // P
 CHUNKS = PARTICLES // CHUNK
 ROW_TILES = PARTICLES // P
+ALPHA_ROW = BATCH * ROW_TILES
+BETA_ROW = ALPHA_ROW + 1
+LOADS = (((0, 1), (1, 1), (2, 2)), ((0, 4),))
 
 FLOPS = 2 * BATCH * PARTICLES * PARTICLES * FEATURES
 
@@ -46,11 +49,6 @@ def tile_qcdawareold_kernel(tc, emb, alpha_p, beta_p, out):
         ident_bf16 = keep.tile([P, P], BF16, name="ident_bf16")
         make_identity(nc, ident_bf16[:])
 
-        alpha_bf16 = keep.tile([P, 1], BF16, name="alpha_bf16")
-        nc.scalar.dma_start(out=alpha_bf16[:], in_=alpha_p.rearrange("a b -> (a b)").partition_broadcast(P))
-        beta_bf16 = keep.tile([P, 1], BF16, name="beta_bf16")
-        nc.scalar.dma_start(out=beta_bf16[:], in_=beta_p.rearrange("a b c -> (a b c)").partition_broadcast(P))
-
         momentum_rows = keep.tile([P, P], BF16, name="momentum_rows")
         nc.vector.memset(momentum_rows[:], 0.0)
         for b in range(BATCH):
@@ -59,19 +57,28 @@ def tile_qcdawareold_kernel(tc, emb, alpha_p, beta_p, out):
                 in_=emb[b, MOMENTUM_FEATURE, :].rearrange("(t p) -> t p", p=P),
             )
 
+        nc.scalar.dma_start(out=momentum_rows[ALPHA_ROW : ALPHA_ROW + 1, 0:1], in_=alpha_p)
+        nc.scalar.dma_start(
+            out=momentum_rows[BETA_ROW : BETA_ROW + 1, 0:1], in_=beta_p.rearrange("a b c -> (a b) c")
+        )
+
         raw = [[None] * CHUNKS for b in range(BATCH)]
         for b in range(BATCH):
             rows = emb[b].rearrange("(p t) w -> p t w", t=PACK)
-            for c in range(CHUNKS):
-                raw[b][c] = keep.tile([P, PACK, CHUNK], BF16, name="raw%d%d" % (b, c))
-                nc.sync.dma_start(out=raw[b][c][:], in_=rows[:, :, c * CHUNK : (c + 1) * CHUNK])
+            for first, count in LOADS[b]:
+                piece = keep.tile([P, PACK, count * CHUNK], BF16, name="raw%d%d" % (b, first))
+                nc.sync.dma_start(out=piece[:], in_=rows[:, :, first * CHUNK : (first + count) * CHUNK])
+                for c in range(first, first + count):
+                    raw[b][c] = piece[:, :, (c - first) * CHUNK : (c - first + 1) * CHUNK]
 
+        scalars = psum_prepare.tile([P, P], BF16, name="scalars", tag="prepare")
+        nc.tensor.transpose(scalars[:], momentum_rows[:, 0:1].to_broadcast([P, P]), ident_bf16[:])
         two_alpha = keep.tile([P, 1], F32, name="two_alpha")
         nc.vector.tensor_scalar(
-            out=two_alpha[:], in0=alpha_bf16[:], scalar1=2.0, scalar2=None, op0=ALU.mult
+            out=two_alpha[:], in0=scalars[:, ALPHA_ROW : ALPHA_ROW + 1], scalar1=2.0, scalar2=None, op0=ALU.mult
         )
         beta_f32 = keep.tile([P, 1], F32, name="beta_f32")
-        nc.vector.tensor_copy(out=beta_f32[:], in_=beta_bf16[:])
+        nc.vector.tensor_copy(out=beta_f32[:], in_=scalars[:, BETA_ROW : BETA_ROW + 1])
         two_beta_sq = keep.tile([P, 1], F32, name="two_beta_sq")
         nc.vector.tensor_scalar(
             out=two_beta_sq[:], in0=beta_f32[:], scalar1=beta_f32[:, 0:1], scalar2=2.0,

@@ -24,7 +24,7 @@ CHUNKS = PARTICLES // CHUNK
 ROW_TILES = PARTICLES // P
 ALPHA_ROW = BATCH * ROW_TILES
 BETA_ROW = ALPHA_ROW + 1
-LOADS = (((0, 1), (1, 1), (2, 2)), ((0, 4),))
+LOADS = (((0, 1), (1, 1), (2, 1), (3, 1)), ((0, 1), (1, 1), (2, 1), (3, 1)))
 
 FLOPS = 2 * BATCH * PARTICLES * PARTICLES * FEATURES
 
@@ -71,7 +71,7 @@ def tile_qcdawareold_kernel(tc, emb, alpha_p, beta_p, out):
                 for c in range(first, first + count):
                     raw[b][c] = piece[:, :, (c - first) * CHUNK : (c - first + 1) * CHUNK]
 
-        scalars = psum_prepare.tile([P, P], BF16, name="scalars", tag="prepare")
+        scalars = psum_p_row.tile([P, P], BF16, name="scalars", tag="p_row")
         nc.tensor.transpose(scalars[:], momentum_rows[:, 0:1].to_broadcast([P, P]), ident_bf16[:])
         two_alpha = keep.tile([P, 1], F32, name="two_alpha")
         nc.vector.tensor_scalar(
@@ -84,7 +84,7 @@ def tile_qcdawareold_kernel(tc, emb, alpha_p, beta_p, out):
             out=two_beta_sq[:], in0=beta_f32[:], scalar1=beta_f32[:, 0:1], scalar2=2.0,
             op0=ALU.mult, op1=ALU.mult,
         )
-        momentum_cols = psum_prepare.tile([P, P], BF16, name="momentum_cols", tag="prepare")
+        momentum_cols = psum_p_row.tile([P, P], BF16, name="momentum_cols", tag="p_row")
         nc.tensor.transpose(momentum_cols[:], momentum_rows[:], ident_bf16[:])
         log_momentum = keep.tile([P, BATCH * ROW_TILES], F32, name="log_momentum")
         nc.scalar.activation(out=log_momentum[:], in_=momentum_cols[:, 0 : BATCH * ROW_TILES], func=ACT.Ln)
@@ -150,7 +150,7 @@ def tile_qcdawareold_kernel(tc, emb, alpha_p, beta_p, out):
             spread(h_bank, lambda q: h_col[b][c][:, q : q + 1])
             h_row[b][c] = keep.tile([P, CHUNK], F32, name="h_row%d%d" % (b, c))
             nc.scalar.copy(out=h_row[b][c][:], in_=h_bank[:])
-            p_row[b][c] = psum_p_row.tile([P, CHUNK], F32, name="p_row")
+            p_row[b][c] = psum_p_row.tile([P, CHUNK], F32, name="p_row", tag="p_row")
             spread(p_row[b][c], lambda q: p_col[:, first + q : first + q + 1])
 
         def half_distance(b, a, r, c, lo):

from contextlib import ExitStack

from concourse import mybir
from concourse.masks import make_identity

F32 = mybir.dt.float32
BF16 = mybir.dt.bfloat16
U32 = mybir.dt.uint32
U8 = mybir.dt.uint8
FP8X4 = mybir.dt.float8_e4m3fn_x4
ALU = mybir.AluOpType
ACT = mybir.ActivationFunctionType

BATCH = 2
FEATURES = 512
PARTICLES = 2048
MOMENTUM_FEATURE = 4

P = 128
PACK = 4
CHUNK = 512
BLOCKS = CHUNK // P
CHUNKS = PARTICLES // CHUNK
ROW_TILES = PARTICLES // P
ALPHA_ROW = BATCH * ROW_TILES
BETA_ROW = ALPHA_ROW + 1
LOADS = (((0, 1), (1, 1), (2, 1), (3, 1)), ((0, 1), (1, 1), (2, 1), (3, 1)))

FLOPS = 2 * BATCH * PARTICLES * PARTICLES * FEATURES

assert FEATURES == P * PACK


def tile_qcdawareold_kernel(tc, emb, alpha_p, beta_p, out):
    nc = tc.nc
    with ExitStack() as ctx:
        keep = ctx.enter_context(tc.tile_pool(name="keep", bufs=1))
        stage = ctx.enter_context(tc.tile_pool(name="stage", bufs=1))
        exponents = ctx.enter_context(tc.tile_pool(name="exponents", bufs=3 * BLOCKS))
        results = ctx.enter_context(tc.tile_pool(name="results", bufs=8))
        mirrors = ctx.enter_context(tc.tile_pool(name="mirrors", bufs=4 * BLOCKS))
        psum_gram = ctx.enter_context(tc.psum_pool(name="psum_gram", bufs=2))
        psum_mirror = ctx.enter_context(tc.psum_pool(name="psum_mirror", bufs=3))
        psum_prepare = ctx.enter_context(tc.psum_pool(name="psum_prepare", bufs=1))
        psum_p_row = ctx.enter_context(tc.psum_pool(name="psum_p_row", bufs=2))

        ident_f32 = keep.tile([P, P], F32, name="ident_f32")
        make_identity(nc, ident_f32[:])
        ident_bf16 = keep.tile([P, P], BF16, name="ident_bf16")
        make_identity(nc, ident_bf16[:])

        momentum_rows = keep.tile([P, P], BF16, name="momentum_rows")
        nc.vector.memset(momentum_rows[:], 0.0)
        for b in range(BATCH):
            nc.scalar.dma_start(
                out=momentum_rows[b * ROW_TILES : (b + 1) * ROW_TILES, :],
                in_=emb[b, MOMENTUM_FEATURE, :].rearrange("(t p) -> t p", p=P),
            )

        nc.scalar.dma_start(out=momentum_rows[ALPHA_ROW : ALPHA_ROW + 1, 0:1], in_=alpha_p)
        nc.scalar.dma_start(
            out=momentum_rows[BETA_ROW : BETA_ROW + 1, 0:1], in_=beta_p.rearrange("a b c -> (a b) c")
        )

        raw = [[None] * CHUNKS for b in range(BATCH)]
        for b in range(BATCH):
            rows = emb[b].rearrange("(p t) w -> p t w", t=PACK)
            for first, count in LOADS[b]:
                piece = keep.tile([P, PACK, count * CHUNK], BF16, name="raw%d%d" % (b, first))
                nc.sync.dma_start(out=piece[:], in_=rows[:, :, first * CHUNK : (first + count) * CHUNK])
                for c in range(first, first + count):
                    raw[b][c] = piece[:, :, (c - first) * CHUNK : (c - first + 1) * CHUNK]

        scalars = psum_p_row.tile([P, P], BF16, name="scalars", tag="p_row")
        nc.tensor.transpose(scalars[:], momentum_rows[:, 0:1].to_broadcast([P, P]), ident_bf16[:])
        two_alpha = keep.tile([P, 1], F32, name="two_alpha")
        nc.vector.tensor_scalar(
            out=two_alpha[:], in0=scalars[:, ALPHA_ROW : ALPHA_ROW + 1], scalar1=2.0, scalar2=None, op0=ALU.mult
        )
        beta_f32 = keep.tile([P, 1], F32, name="beta_f32")
        nc.vector.tensor_copy(out=beta_f32[:], in_=scalars[:, BETA_ROW : BETA_ROW + 1])
        two_beta_sq = keep.tile([P, 1], F32, name="two_beta_sq")
        nc.vector.tensor_scalar(
            out=two_beta_sq[:], in0=beta_f32[:], scalar1=beta_f32[:, 0:1], scalar2=2.0,
            op0=ALU.mult, op1=ALU.mult,
        )
        momentum_cols = psum_p_row.tile([P, P], BF16, name="momentum_cols", tag="p_row")
        nc.tensor.transpose(momentum_cols[:], momentum_rows[:], ident_bf16[:])
        log_momentum = keep.tile([P, BATCH * ROW_TILES], F32, name="log_momentum")
        nc.scalar.activation(out=log_momentum[:], in_=momentum_cols[:, 0 : BATCH * ROW_TILES], func=ACT.Ln)
        power = keep.tile([P, BATCH * ROW_TILES], F32, name="power")
        nc.scalar.activation(out=power[:], in_=log_momentum[:], func=ACT.Exp, scale=two_alpha[:, 0:1])
        p_col = keep.tile([P, BATCH * ROW_TILES], F32, name="p_col")
        nc.vector.tensor_scalar(
            out=p_col[:], in0=power[:], scalar1=two_beta_sq[:, 0:1], scalar2=None, op0=ALU.mult
        )

        codes = [[None] * CHUNKS for b in range(BATCH)]
        scales = [[None] * CHUNKS for b in range(BATCH)]
        h_col = [[None] * CHUNKS for b in range(BATCH)]
        h_row = [[None] * CHUNKS for b in range(BATCH)]
        p_row = [[None] * CHUNKS for b in range(BATCH)]

        def spread(bank, column_of_block):
            for q in range(BLOCKS):
                nc.tensor.transpose(
                    bank[:, q * P : (q + 1) * P], column_of_block(q).to_broadcast([P, P]), ident_f32[:]
                )

        def prepare_chunk(b, c):
            source = raw[b][c]
            grouped = stage.tile([P, CHUNK, PACK], BF16, name="grouped", align_bytes=64)
            if (b, c) == (0, 0):
                nc.vector.tensor_copy(
                    out=grouped[:].rearrange("p (c i) t -> p c t i", i=4),
                    in_=source[:].rearrange("p t (c i) -> p c t i", i=4),
                )
            else:
                nc.gpsimd.tensor_scalar(
                    out=grouped[:], in0=source[:].rearrange("p t w -> p w t"), scalar1=1.0, scalar2=0.0,
                    op0=ALU.mult, op1=ALU.add,
                )

            norms = psum_prepare.tile([P, CHUNK], F32, name="norms", tag="prepare")
            for q in range(BLOCKS):
                for t in range(PACK):
                    block = source[:, t, q * P : (q + 1) * P]
                    nc.tensor.matmul(
                        norms[:, q * P : (q + 1) * P], lhsT=block, rhs=block,
                        start=(t == 0), stop=(t == PACK - 1),
                    )
            h_col[b][c] = keep.tile([P, BLOCKS], F32, name="h_col%d%d" % (b, c))
            masked = stage.tile([P, CHUNK], F32, name="masked")
            for q in range(BLOCKS):
                nc.vector.scalar_tensor_tensor(
                    out=masked[:, q * P : (q + 1) * P], in0=norms[:, q * P : (q + 1) * P], scalar=0.5,
                    in1=ident_f32[:], op0=ALU.mult, op1=ALU.mult, accum_out=h_col[b][c][:, q : q + 1],
                )

            codes[b][c] = keep.tile([P, CHUNK], U32, name="codes%d%d" % (b, c), align_bytes=64)
            scales[b][c] = keep.tile([P, CHUNK], U8, name="scales%d%d" % (b, c), align_bytes=64)
            nc.vector.quantize_mx(
                out=codes[b][c][:].bitcast(FP8X4),
                scales=scales[b][c][:],
                in_=grouped[:].rearrange("p w t -> p (w t)"),
            )

            first = b * ROW_TILES + c * BLOCKS
            h_bank = psum_prepare.tile([P, CHUNK], F32, name="h_bank", tag="prepare")
            spread(h_bank, lambda q: h_col[b][c][:, q : q + 1])
            h_row[b][c] = keep.tile([P, CHUNK], F32, name="h_row%d%d" % (b, c))
            nc.scalar.copy(out=h_row[b][c][:], in_=h_bank[:])
            p_row[b][c] = psum_p_row.tile([P, CHUNK], F32, name="p_row", tag="p_row")
            spread(p_row[b][c], lambda q: p_col[:, first + q : first + q + 1])

        def half_distance(b, a, r, c, lo):
            gram = psum_gram.tile([P, CHUNK], F32, name="gram")
            nc.tensor.matmul_mx(
                out=gram[:],
                lhsT=codes[b][a][:, r * P : (r + 1) * P].bitcast(FP8X4),
                lhsT_scale=scales[b][a][:, r * P : (r + 1) * P],
                rhs=codes[b][c][:].bitcast(FP8X4),
                rhs_scale=scales[b][c][:],
                start=True,
                stop=True,
            )
            x = exponents.tile([P, CHUNK], F32, name="x")
            nc.vector.scalar_tensor_tensor(
                out=x[:, lo:], in0=gram[:, lo:], scalar=h_col[b][a][:, r : r + 1], in1=h_row[b][c][:, lo:],
                op0=ALU.subtract, op1=ALU.subtract,
            )
            return x

        def weigh(b, a, r, c, lo, x):
            i = b * ROW_TILES + a * BLOCKS + r
            nc.vector.scalar_tensor_tensor(
                out=x[:, lo:], in0=p_row[b][c][:, lo:], scalar=p_col[:, i : i + 1], in1=x[:, lo:],
                op0=ALU.min, op1=ALU.mult,
            )

        def unit(b, a, c, mirror, at):
            diagonal = a == c

            def finish(r, x):
                lo = r * P if diagonal else 0
                weigh(b, a, r, c, lo, x)
                if diagonal:
                    nc.scalar.activation(out=mirror[r][:, at + lo : at + CHUNK], in_=x[:, lo:], func=ACT.Exp)
                else:
                    direct = results.tile([P, CHUNK], F32, name="direct")
                    nc.scalar.activation(out=direct[:], in_=x[:], func=ACT.Exp)
                    row0 = (a * BLOCKS + r) * P
                    nc.sync.dma_start(out=out[b, row0 : row0 + P, c * CHUNK : (c + 1) * CHUNK], in_=direct[:])

            xs = []
            for r in range(BLOCKS):
                xs.append(half_distance(b, a, r, c, r * P if diagonal else 0))
                if r > 0:
                    finish(r - 1, xs[r - 1])
            finish(BLOCKS - 1, xs[BLOCKS - 1])

            for q in range(1 if diagonal else 0, BLOCKS):
                sources = q if diagonal else BLOCKS
                flipped = psum_mirror.tile([P, CHUNK], F32, name="flipped")
                for r in range(sources):
                    nc.tensor.transpose(
                        flipped[:, r * P : (r + 1) * P], xs[r][:, q * P : (q + 1) * P], ident_f32[:]
                    )
                nc.scalar.activation(
                    out=mirror[q][:, at : at + sources * P], in_=flipped[:, 0 : sources * P], func=ACT.Exp
                )

        def column_step(b, c):
            for a in range(c + 1):
                if a % 2 == 0:
                    mirror = [mirrors.tile([P, 2 * CHUNK], F32, name="mirror") for q in range(BLOCKS)]
                unit(b, a, c, mirror, (a % 2) * CHUNK)
                if a % 2 == 1 or a == c:
                    col0 = (a - a % 2) * CHUNK
                    width = (a % 2 + 1) * CHUNK
                    for q in range(BLOCKS):
                        row0 = (c * BLOCKS + q) * P
                        nc.sync.dma_start(
                            out=out[b, row0 : row0 + P, col0 : col0 + width], in_=mirror[q][:, 0:width]
                        )

        steps = [(b, c) for b in range(BATCH) for c in range(CHUNKS)]
        prepare_chunk(*steps[0])
        for s in range(len(steps)):
            if s + 1 < len(steps):
                prepare_chunk(*steps[s + 1])
            column_step(*steps[s])
